import numpy as np
import ml_dtypes


def mxq(x, axis, fmt="e4m3"):
    dtype, down = {"e4m3": (ml_dtypes.float8_e4m3fn, 7), "e5m2": (ml_dtypes.float8_e5m2, 14)}[fmt]
    v = np.moveaxis(np.asarray(x, np.float32).astype(ml_dtypes.bfloat16).astype(np.float64), axis, -1)
    blocks = v.reshape(v.shape[:-1] + (-1, 32))
    amax = np.abs(blocks).max(-1, keepdims=True)
    byte = np.maximum(np.where(amax > 0, np.frexp(amax)[1] - 1 + 127, 0) - down, 1)
    scale = np.exp2(byte - 127.0)
    codes = (blocks / scale).astype(np.float32).astype(dtype).astype(np.float64)
    return np.moveaxis((codes * scale).reshape(v.shape), -1, axis)


WIDE = False


def mx_kscale(k):
    if not WIDE:
        return np.ones(k)
    levels = np.array([10, -10, 5, -5, 0])
    a = np.random.permutation(np.resize(levels, k // 512 * 4)).reshape(k // 512, 4)
    idx = np.arange(k)
    return np.exp2(a[idx // 512, idx % 128 // 32])


BF16 = ml_dtypes.bfloat16


def bf(x):
    return np.asarray(x, np.float32).astype(BF16)


def f64(x):
    return np.asarray(x).astype(np.float64)


B, C, PS, G, E = 24, 3, 64, 4, 512
NP = G * G
M1 = NP // 2
K2 = 2 * E


def setup_inputs():
    t = mx_kscale(K2)[:E]
    tt = np.concatenate([t, t])
    return {"h1": bf(np.random.standard_normal((B, NP, M1, E)) * t),
            "cross_w": bf(np.random.standard_normal((E, K2)) / np.sqrt(K2) * t[:, None] / tt[None, :]),
            "cross_b": bf(np.random.standard_normal(E) * 0.3 * t)}


def reference(h1, cross_w, cross_b):
    wq = mxq(f64(cross_w), 1, "e4m3")
    bias = f64(cross_b)
    g1 = f64(h1).reshape(B, NP, M1 // 2, K2)
    h2 = (mxq(g1, 3, "e4m3") @ wq.T) + bias
    g2 = h2.reshape(B, NP, M1 // 4, K2)
    return (mxq(g2, 3, "e4m3") @ wq.T) + bias

@@ -1,0 +1,241 @@
+from contextlib import ExitStack
+
+import concourse.masks as masks
+import concourse.mybir as mybir
+
+F32 = mybir.dt.float32
+BF16 = mybir.dt.bfloat16
+I32 = mybir.dt.int32
+U32 = mybir.dt.uint32
+U8 = mybir.dt.uint8
+FP8X4 = mybir.dt.float8_e4m3fn_x4
+
+P = 128
+PACK = 4
+E = 512
+K2 = 2 * E
+PASSES = K2 // (P * PACK)
+ROW_WORDS = K2 // 2
+OUT_ROWS = 768
+CHUNK = P
+CHUNKS = OUT_ROWS // CHUNK
+COLS1 = 2 * CHUNK
+
+FLOPS = 2 * (2 * OUT_ROWS) * K2 * E + 2 * OUT_ROWS * K2 * E
+
+
+def tile_simplemodel_pc_kernel(tc, h1, cross_w, cross_b, out):
+    nc = tc.nc
+
+    x_dram = h1.rearrange("b i (h s) e -> (b i h) (s e)", s=4)
+    w_dram = cross_w.rearrange("(u p e) k -> u p (e k)", u=2, e=2)
+    out_dram = out.rearrange("b i h e -> (b i h) e")
+
+    with ExitStack() as ctx:
+        const = ctx.enter_context(tc.tile_pool(name="const", bufs=1))
+        xin = ctx.enter_context(tc.tile_pool(name="xin", bufs=CHUNKS))
+        work = ctx.enter_context(tc.tile_pool(name="work", bufs=3))
+        psum_t = ctx.enter_context(tc.psum_pool(name="psum_t", bufs=4))
+        psum_h = ctx.enter_context(tc.psum_pool(name="psum_h", bufs=2))
+        psum_o = ctx.enter_context(tc.psum_pool(name="psum_o", bufs=2))
+        ctx.enter_context(tc.manual_schedule())
+
+        w_sb = const.tile([P, PACK * K2], BF16)
+        x_sb = []
+        for c in range(CHUNKS):
+            x_rows = xin.tile([P, 2 * K2], BF16)
+            x_sb.append(x_rows)
+
+        def load_x(c):
+            nc.sync.dma_start(out=x_sb[c][:], in_=x_dram[c * CHUNK : (c + 1) * CHUNK, :])
+
+        load_x(0)
+        for u in range(2):
+            nc.sync.dma_start(out=w_sb[:, u * 2 * K2 : (u + 1) * 2 * K2], in_=w_dram[u])
+        for c in range(1, CHUNKS):
+            load_x(c)
+
+        ident = const.tile([P, P], F32)
+        masks.make_identity(nc, ident[:])
+        ones = const.tile([P, P], BF16)
+        nc.vector.memset(ones[:], 1.0)
+        bias_row0 = const.tile([P, E], BF16)
+        nc.vector.memset(bias_row0[:].bitcast(I32), 0)
+        nc.scalar.dma_start(out=bias_row0[0:1, :], in_=cross_b.unsqueeze(0))
+
+        w_grouped = const.tile([P, PASSES * E * PACK], BF16, align_bytes=64)
+        w_codes = const.tile([P, PASSES, E], U32, align_bytes=64)
+        w_scales = const.tile([P, PASSES, E], U8, align_bytes=64)
+        bias_rows = const.tile([P, E], F32)
+        bias_cols = const.tile([P, PACK], F32)
+
+        def transpose_rows(words):
+            bank = psum_t.tile([P, PASSES * 2, P], F32)
+            for block in range(PASSES * 2):
+                nc.tensor.transpose(bank[:, block, :], words[:, block * P : (block + 1) * P], ident[:])
+            return bank
+
+        def copy_grouped(copy, grouped, columns, first, bank):
+            words = grouped[:].bitcast(F32).rearrange("p (g c u) -> p g c u", g=PASSES, c=columns)
+            copy(
+                out=words[:, :, first : first + P, :],
+                in_=bank[:].rearrange("p (g u) r -> p g r u", g=PASSES),
+            )
+
+        t_banks, x_grouped, x_codes, x_scales = {}, {}, {}, {}
+        h_banks, h2t, g2_grouped, g2_codes, g2_scales, o_banks = {}, {}, {}, {}, {}, {}
+
+        def transpose_x(c):
+            words = x_sb[c][:].bitcast(F32)
+            t_banks[c] = [
+                transpose_rows(words[:, j * ROW_WORDS : (j + 1) * ROW_WORDS]) for j in range(2)
+            ]
+
+        def group_x(c):
+            grouped = work.tile([P, PASSES * COLS1 * PACK], BF16, align_bytes=64, name="x_grouped")
+            for j in range(2):
+                copy_grouped(nc.scalar.copy, grouped, COLS1, j * P, t_banks[c][j])
+            x_grouped[c] = grouped
+
+        def quantise_x(c):
+            codes = work.tile([P, PASSES, COLS1], U32, align_bytes=64, name="x_codes")
+            scales = work.tile([P, PASSES, COLS1], U8, align_bytes=64, name="x_scales")
+            nc.vector.quantize_mx(
+                out=codes[:].rearrange("p g c -> p (g c)").bitcast(FP8X4),
+                scales=scales[:].rearrange("p g c -> p (g c)"),
+                in_=x_grouped[c][:],
+            )
+            x_codes[c], x_scales[c] = codes, scales
+
+        def weight_tile_in(t):
+            words = w_sb[:].bitcast(F32)
+            bank = transpose_rows(words[:, t * ROW_WORDS : (t + 1) * ROW_WORDS])
+            copy = nc.vector.tensor_copy if t % 2 == 0 else nc.scalar.copy
+            copy_grouped(copy, w_grouped, E, t * P, bank)
+
+        def quantise_w(t):
+            columns = slice(t * P, (t + 1) * P)
+            grouped = w_grouped[:].rearrange("p (g c t) -> p g c t", g=PASSES, t=PACK)
+            for g in range(PASSES):
+                nc.vector.quantize_mx(
+                    out=w_codes[:, g, columns].bitcast(FP8X4),
+                    scales=w_scales[:, g, columns],
+                    in_=grouped[:, g, columns, :].rearrange("p c t -> p (c t)"),
+                )
+
+        def level_one(c):
+            h_banks[c] = []
+            for pair in range(PACK // 2):
+                bank = psum_h.tile([P, 2, COLS1], F32, name="h_bank")
+                for half in range(2):
+                    columns = slice((2 * pair + half) * P, (2 * pair + half + 1) * P)
+                    for g in range(PASSES):
+                        nc.tensor.matmul_mx(
+                            out=bank[:, half, :],
+                            lhsT=w_codes[:, g, columns].bitcast(FP8X4),
+                            lhsT_scale=w_scales[:, g, columns],
+                            rhs=x_codes[c][:, g, :].bitcast(FP8X4),
+                            rhs_scale=x_scales[c][:, g, :],
+                            start=(g == 0),
+                            stop=(g == PASSES - 1),
+                        )
+                h_banks[c].append(bank)
+
+        def add_bias_one(c):
+            rounded = work.tile([P, PACK, COLS1], BF16, name="h2t")
+            for t in range(PACK):
+                nc.scalar.activation(
+                    out=rounded[:, t, :],
+                    in_=h_banks[c][t // 2][:, t % 2, :],
+                    func=mybir.ActivationFunctionType.Identity,
+                    bias=bias_cols[:, t : t + 1],
+                    scale=1.0,
+                )
+            h2t[c] = rounded
+
+        def group_g2(c):
+            grouped = work.tile([P, COLS1 * PACK], BF16, align_bytes=64, name="g2_grouped")
+            nc.vector.tensor_copy(
+                out=grouped[:].rearrange("p (c t) -> p c t", t=PACK),
+                in_=h2t[c][:].rearrange("p t c -> p c t"),
+            )
+            g2_grouped[c] = grouped
+
+        def quantise_g2(c):
+            codes = work.tile([P, PASSES, CHUNK], U32, align_bytes=64, name="g2_codes")
+            scales = work.tile([P, PASSES, CHUNK], U8, align_bytes=64, name="g2_scales")
+            nc.vector.quantize_mx(
+                out=codes[:].rearrange("p g r -> p (g r)").bitcast(FP8X4),
+                scales=scales[:].rearrange("p g r -> p (g r)"),
+                in_=g2_grouped[c][:],
+            )
+            g2_codes[c], g2_scales[c] = codes, scales
+
+        def level_two(c):
+            bank = psum_o.tile([P, E], F32, name="o_bank")
+            for g in range(PASSES):
+                nc.tensor.matmul_mx(
+                    out=bank[:],
+                    lhsT=g2_codes[c][:, g, :].bitcast(FP8X4),
+                    lhsT_scale=g2_scales[c][:, g, :],
+                    rhs=w_codes[:, g, :].bitcast(FP8X4),
+                    rhs_scale=w_scales[:, g, :],
+                    start=(g == 0),
+                    stop=(g == PASSES - 1),
+                )
+            o_banks[c] = bank
+
+        def finish(c):
+            result = work.tile([P, E], F32, name="result")
+            nc.vector.tensor_tensor(
+                out=result[:].rearrange("p (u i e) -> p u i e", u=2, e=2),
+                in0=o_banks[c][:].rearrange("p (u e i) -> p u i e", u=2, e=2),
+                in1=bias_rows[:].rearrange("p (u i e) -> p u i e", u=2, e=2),
+                op=mybir.AluOpType.add,
+            )
+            nc.sync.dma_start(out=out_dram[c * CHUNK : (c + 1) * CHUNK, :], in_=result[:])
+
+        transpose_x(0)
+        group_x(0)
+
+        spread = psum_o.tile([P, E], F32, tag="o_bank")
+        nc.tensor.matmul(out=spread[:], lhsT=ones[:], rhs=bias_row0[:], start=True, stop=True)
+        nc.scalar.copy(out=bias_rows[:], in_=spread[:])
+        turned = psum_h.tile([P, 2 * P], F32, tag="h_bank")
+        for u in range(2):
+            nc.tensor.transpose(
+                turned[:, u * P : (u + 1) * P],
+                bias_row0[:].bitcast(F32)[:, u * P : (u + 1) * P],
+                ident[:],
+            )
+        nc.vector.tensor_copy(
+            out=bias_cols[:].rearrange("p (u e) -> p u e", u=2),
+            in_=turned[:].bitcast(BF16).rearrange("p (u c) -> p u c", u=2)[:, :, 0:2],
+        )
+
+        weight_tile_in(0)
+        quantise_x(0)
+        for t in range(1, PACK):
+            weight_tile_in(t)
+            quantise_w(t - 1)
+        transpose_x(1)
+        group_x(1)
+        quantise_w(PACK - 1)
+
+        for i in range(CHUNKS + 2):
+            if 0 <= i - 1 < CHUNKS:
+                quantise_g2(i - 1)
+            if i < CHUNKS:
+                level_one(i)
+                add_bias_one(i)
+            if i + 2 < CHUNKS:
+                transpose_x(i + 2)
+                group_x(i + 2)
+            if 0 <= i - 1 < CHUNKS:
+                level_two(i - 1)
+            if 0 <= i - 2 < CHUNKS:
+                finish(i - 2)
+            if i + 1 < CHUNKS:
+                quantise_x(i + 1)
+            if i < CHUNKS:
+                group_g2(i)

@@ -28,17 +28,22 @@ def tile_simplemodel_pc_kernel(tc, h1, cross_w, cross_b, out):
     nc = tc.nc
 
     x_dram = h1.rearrange("b i (h s) e -> (b i h) (s e)", s=4)
-    w_dram = cross_w.rearrange("(u p e) k -> u p (e k)", u=2, e=2)
+    w_dram = cross_w.rearrange("(u p e) k -> u e p k", u=2, e=2)
     out_dram = out.rearrange("b i h e -> (b i h) e")
 
     with ExitStack() as ctx:
         const = ctx.enter_context(tc.tile_pool(name="const", bufs=1))
         xin = ctx.enter_context(tc.tile_pool(name="xin", bufs=CHUNKS))
         work = ctx.enter_context(tc.tile_pool(name="work", bufs=3))
-        psum_t = ctx.enter_context(tc.psum_pool(name="psum_t", bufs=4))
-        psum_h = ctx.enter_context(tc.psum_pool(name="psum_h", bufs=2))
-        psum_o = ctx.enter_context(tc.psum_pool(name="psum_o", bufs=2))
+        psum = ctx.enter_context(tc.psum_pool(name="psum", bufs=8))
         ctx.enter_context(tc.manual_schedule())
+
+        ident = const.tile([P, P], F32)
+        masks.make_identity(nc, ident[:])
+        ones = const.tile([P, P], BF16)
+        nc.vector.memset(ones[:], 1.0)
+        bias_row0 = const.tile([P, E], BF16)
+        nc.vector.memset(bias_row0[:].bitcast(I32), 0)
 
         w_sb = const.tile([P, PACK * K2], BF16)
         x_sb = []
@@ -47,21 +52,23 @@ def tile_simplemodel_pc_kernel(tc, h1, cross_w, cross_b, out):
             x_sb.append(x_rows)
 
         def load_x(c):
-            nc.sync.dma_start(out=x_sb[c][:], in_=x_dram[c * CHUNK : (c + 1) * CHUNK, :])
+            for j in range(2):
+                k_range = slice(j * K2, (j + 1) * K2)
+                nc.sync.dma_start(
+                    out=x_sb[c][:, k_range], in_=x_dram[c * CHUNK : (c + 1) * CHUNK, k_range]
+                )
+
+        def load_w(t):
+            nc.sync.dma_start(out=w_sb[:, t * K2 : (t + 1) * K2], in_=w_dram[t // 2, t % 2])
 
         load_x(0)
-        for u in range(2):
-            nc.sync.dma_start(out=w_sb[:, u * 2 * K2 : (u + 1) * 2 * K2], in_=w_dram[u])
+        load_w(0)
+        load_w(1)
+        nc.sync.dma_start(out=bias_row0[0:1, :], in_=cross_b.unsqueeze(0))
+        load_w(2)
+        load_w(3)
         for c in range(1, CHUNKS):
             load_x(c)
-
-        ident = const.tile([P, P], F32)
-        masks.make_identity(nc, ident[:])
-        ones = const.tile([P, P], BF16)
-        nc.vector.memset(ones[:], 1.0)
-        bias_row0 = const.tile([P, E], BF16)
-        nc.vector.memset(bias_row0[:].bitcast(I32), 0)
-        nc.scalar.dma_start(out=bias_row0[0:1, :], in_=cross_b.unsqueeze(0))
 
         w_grouped = const.tile([P, PASSES * E * PACK], BF16, align_bytes=64)
         w_codes = const.tile([P, PASSES, E], U32, align_bytes=64)
@@ -70,7 +77,7 @@ def tile_simplemodel_pc_kernel(tc, h1, cross_w, cross_b, out):
         bias_cols = const.tile([P, PACK], F32)
 
         def transpose_rows(words):
-            bank = psum_t.tile([P, PASSES * 2, P], F32)
+            bank = psum.tile([P, PASSES * 2, P], F32, tag="bank")
             for block in range(PASSES * 2):
                 nc.tensor.transpose(bank[:, block, :], words[:, block * P : (block + 1) * P], ident[:])
             return bank
@@ -125,20 +132,19 @@ def tile_simplemodel_pc_kernel(tc, h1, cross_w, cross_b, out):
 
         def level_one(c):
             h_banks[c] = []
-            for pair in range(PACK // 2):
-                bank = psum_h.tile([P, 2, COLS1], F32, name="h_bank")
-                for half in range(2):
-                    columns = slice((2 * pair + half) * P, (2 * pair + half + 1) * P)
-                    for g in range(PASSES):
-                        nc.tensor.matmul_mx(
-                            out=bank[:, half, :],
-                            lhsT=w_codes[:, g, columns].bitcast(FP8X4),
-                            lhsT_scale=w_scales[:, g, columns],
-                            rhs=x_codes[c][:, g, :].bitcast(FP8X4),
-                            rhs_scale=x_scales[c][:, g, :],
-                            start=(g == 0),
-                            stop=(g == PASSES - 1),
-                        )
+            for t in range(PACK):
+                columns = slice(t * P, (t + 1) * P)
+                bank = psum.tile([P, COLS1], F32, tag="bank", name="h_bank")
+                for g in range(PASSES):
+                    nc.tensor.matmul_mx(
+                        out=bank[:],
+                        lhsT=w_codes[:, g, columns].bitcast(FP8X4),
+                        lhsT_scale=w_scales[:, g, columns],
+                        rhs=x_codes[c][:, g, :].bitcast(FP8X4),
+                        rhs_scale=x_scales[c][:, g, :],
+                        start=(g == 0),
+                        stop=(g == PASSES - 1),
+                    )
                 h_banks[c].append(bank)
 
         def add_bias_one(c):
@@ -146,7 +152,7 @@ def tile_simplemodel_pc_kernel(tc, h1, cross_w, cross_b, out):
             for t in range(PACK):
                 nc.scalar.activation(
                     out=rounded[:, t, :],
-                    in_=h_banks[c][t // 2][:, t % 2, :],
+                    in_=h_banks[c][t][:],
                     func=mybir.ActivationFunctionType.Identity,
                     bias=bias_cols[:, t : t + 1],
                     scale=1.0,
@@ -154,25 +160,27 @@ def tile_simplemodel_pc_kernel(tc, h1, cross_w, cross_b, out):
             h2t[c] = rounded
 
         def group_g2(c):
-            grouped = work.tile([P, COLS1 * PACK], BF16, align_bytes=64, name="g2_grouped")
-            nc.vector.tensor_copy(
-                out=grouped[:].rearrange("p (c t) -> p c t", t=PACK),
-                in_=h2t[c][:].rearrange("p t c -> p c t"),
-            )
+            grouped = work.tile([P, PASSES, CHUNK * PACK], BF16, align_bytes=64, name="g2_grouped")
+            for g in range(PASSES):
+                nc.vector.tensor_copy(
+                    out=grouped[:, g, :].rearrange("p (r t) -> p r t", t=PACK),
+                    in_=h2t[c][:, :, g * CHUNK : (g + 1) * CHUNK].rearrange("p t r -> p r t"),
+                )
             g2_grouped[c] = grouped
 
         def quantise_g2(c):
             codes = work.tile([P, PASSES, CHUNK], U32, align_bytes=64, name="g2_codes")
             scales = work.tile([P, PASSES, CHUNK], U8, align_bytes=64, name="g2_scales")
-            nc.vector.quantize_mx(
-                out=codes[:].rearrange("p g r -> p (g r)").bitcast(FP8X4),
-                scales=scales[:].rearrange("p g r -> p (g r)"),
-                in_=g2_grouped[c][:],
-            )
+            for g in range(PASSES):
+                nc.vector.quantize_mx(
+                    out=codes[:, g, :].bitcast(FP8X4),
+                    scales=scales[:, g, :],
+                    in_=g2_grouped[c][:, g, :],
+                )
             g2_codes[c], g2_scales[c] = codes, scales
 
         def level_two(c):
-            bank = psum_o.tile([P, E], F32, name="o_bank")
+            bank = psum.tile([P, E], F32, tag="bank", name="o_bank")
             for g in range(PASSES):
                 nc.tensor.matmul_mx(
                     out=bank[:],
@@ -195,32 +203,36 @@ def tile_simplemodel_pc_kernel(tc, h1, cross_w, cross_b, out):
             )
             nc.sync.dma_start(out=out_dram[c * CHUNK : (c + 1) * CHUNK, :], in_=result[:])
 
+        def spread_bias():
+            spread = psum.tile([P, E], F32, tag="bank")
+            nc.tensor.matmul(out=spread[:], lhsT=ones[:], rhs=bias_row0[:], start=True, stop=True)
+            nc.scalar.copy(out=bias_rows[:], in_=spread[:])
+            turned = psum.tile([P, 2 * P], F32, tag="bank")
+            for u in range(2):
+                nc.tensor.transpose(
+                    turned[:, u * P : (u + 1) * P],
+                    bias_row0[:].bitcast(F32)[:, u * P : (u + 1) * P],
+                    ident[:],
+                )
+            nc.vector.tensor_copy(
+                out=bias_cols[:].rearrange("p (u e) -> p u e", u=2),
+                in_=turned[:].bitcast(BF16).rearrange("p (u c) -> p u c", u=2)[:, :, 0:2],
+            )
+
         transpose_x(0)
         group_x(0)
-
-        spread = psum_o.tile([P, E], F32, tag="o_bank")
-        nc.tensor.matmul(out=spread[:], lhsT=ones[:], rhs=bias_row0[:], start=True, stop=True)
-        nc.scalar.copy(out=bias_rows[:], in_=spread[:])
-        turned = psum_h.tile([P, 2 * P], F32, tag="h_bank")
-        for u in range(2):
-            nc.tensor.transpose(
-                turned[:, u * P : (u + 1) * P],
-                bias_row0[:].bitcast(F32)[:, u * P : (u + 1) * P],
-                ident[:],
-            )
-        nc.vector.tensor_copy(
-            out=bias_cols[:].rearrange("p (u e) -> p u e", u=2),
-            in_=turned[:].bitcast(BF16).rearrange("p (u c) -> p u c", u=2)[:, :, 0:2],
-        )
-
         weight_tile_in(0)
         quantise_x(0)
-        for t in range(1, PACK):
-            weight_tile_in(t)
-            quantise_w(t - 1)
+        weight_tile_in(1)
+        quantise_w(0)
+        spread_bias()
+        weight_tile_in(2)
+        quantise_w(1)
+        weight_tile_in(3)
+        quantise_w(2)
         transpose_x(1)
         group_x(1)
-        quantise_w(PACK - 1)
+        quantise_w(3)
 
         for i in range(CHUNKS + 2):
             if 0 <= i - 1 < CHUNKS:

@@ -13,6 +13,7 @@ FP8X4 = mybir.dt.float8_e4m3fn_x4
 P = 128
 PACK = 4
 E = 512
+HALF_E = E // 2
 K2 = 2 * E
 PASSES = K2 // (P * PACK)
 ROW_WORDS = K2 // 2
@@ -163,8 +164,8 @@ def tile_simplemodel_pc_kernel(tc, h1, cross_w, cross_b, out):
             grouped = work.tile([P, PASSES, CHUNK * PACK], BF16, align_bytes=64, name="g2_grouped")
             for g in range(PASSES):
                 nc.vector.tensor_copy(
-                    out=grouped[:, g, :].rearrange("p (r t) -> p r t", t=PACK),
-                    in_=h2t[c][:, :, g * CHUNK : (g + 1) * CHUNK].rearrange("p t r -> p r t"),
+                    out=grouped[:, g, :].rearrange("p (c i t) -> p c t i", i=4, t=PACK),
+                    in_=h2t[c][:, :, g * CHUNK : (g + 1) * CHUNK].rearrange("p t (c i) -> p c t i", i=4),
                 )
             g2_grouped[c] = grouped
 
@@ -180,28 +181,35 @@ def tile_simplemodel_pc_kernel(tc, h1, cross_w, cross_b, out):
             g2_codes[c], g2_scales[c] = codes, scales
 
         def level_two(c):
-            bank = psum.tile([P, E], F32, tag="bank", name="o_bank")
-            for g in range(PASSES):
-                nc.tensor.matmul_mx(
-                    out=bank[:],
-                    lhsT=g2_codes[c][:, g, :].bitcast(FP8X4),
-                    lhsT_scale=g2_scales[c][:, g, :],
-                    rhs=w_codes[:, g, :].bitcast(FP8X4),
-                    rhs_scale=w_scales[:, g, :],
-                    start=(g == 0),
-                    stop=(g == PASSES - 1),
-                )
-            o_banks[c] = bank
+            o_banks[c] = []
+            for u in range(2):
+                columns = slice(u * HALF_E, (u + 1) * HALF_E)
+                bank = psum.tile([P, HALF_E], F32, tag="bank", name="o_bank")
+                for g in range(PASSES):
+                    nc.tensor.matmul_mx(
+                        out=bank[:],
+                        lhsT=g2_codes[c][:, g, :].bitcast(FP8X4),
+                        lhsT_scale=g2_scales[c][:, g, :],
+                        rhs=w_codes[:, g, columns].bitcast(FP8X4),
+                        rhs_scale=w_scales[:, g, columns],
+                        start=(g == 0),
+                        stop=(g == PASSES - 1),
+                    )
+                o_banks[c].append(bank)
 
         def finish(c):
             result = work.tile([P, E], F32, name="result")
-            nc.vector.tensor_tensor(
-                out=result[:].rearrange("p (u i e) -> p u i e", u=2, e=2),
-                in0=o_banks[c][:].rearrange("p (u e i) -> p u i e", u=2, e=2),
-                in1=bias_rows[:].rearrange("p (u i e) -> p u i e", u=2, e=2),
-                op=mybir.AluOpType.add,
-            )
-            nc.sync.dma_start(out=out_dram[c * CHUNK : (c + 1) * CHUNK, :], in_=result[:])
+            for u in range(2):
+                columns = slice(u * HALF_E, (u + 1) * HALF_E)
+                nc.vector.tensor_tensor(
+                    out=result[:, columns].rearrange("p (i e) -> p i e", e=2),
+                    in0=o_banks[c][u][:].rearrange("p (e i) -> p i e", e=2),
+                    in1=bias_rows[:, columns].rearrange("p (i e) -> p i e", e=2),
+                    op=mybir.AluOpType.add,
+                )
+                nc.sync.dma_start(
+                    out=out_dram[c * CHUNK : (c + 1) * CHUNK, columns], in_=result[:, columns]
+                )
 
         def spread_bias():
             spread = psum.tile([P, E], F32, tag="bank")
@@ -237,6 +245,8 @@ def tile_simplemodel_pc_kernel(tc, h1, cross_w, cross_b, out):
         for i in range(CHUNKS + 2):
             if 0 <= i - 1 < CHUNKS:
                 quantise_g2(i - 1)
+            if 0 <= i - 2 < CHUNKS:
+                finish(i - 2)
             if i < CHUNKS:
                 level_one(i)
                 add_bias_one(i)
@@ -245,8 +255,6 @@ def tile_simplemodel_pc_kernel(tc, h1, cross_w, cross_b, out):
                 group_x(i + 2)
             if 0 <= i - 1 < CHUNKS:
                 level_two(i - 1)
-            if 0 <= i - 2 < CHUNKS:
-                finish(i - 2)
             if i + 1 < CHUNKS:
                 quantise_x(i + 1)
             if i < CHUNKS:

@@ -37,7 +37,6 @@ def tile_simplemodel_pc_kernel(tc, h1, cross_w, cross_b, out):
         xin = ctx.enter_context(tc.tile_pool(name="xin", bufs=CHUNKS))
         work = ctx.enter_context(tc.tile_pool(name="work", bufs=3))
         psum = ctx.enter_context(tc.psum_pool(name="psum", bufs=8))
-        ctx.enter_context(tc.manual_schedule())
 
         ident = const.tile([P, P], F32)
         masks.make_identity(nc, ident[:])

from contextlib import ExitStack

import concourse.masks as masks
import concourse.mybir as mybir

F32 = mybir.dt.float32
BF16 = mybir.dt.bfloat16
I32 = mybir.dt.int32
U32 = mybir.dt.uint32
U8 = mybir.dt.uint8
FP8X4 = mybir.dt.float8_e4m3fn_x4

P = 128
PACK = 4
E = 512
HALF_E = E // 2
K2 = 2 * E
PASSES = K2 // (P * PACK)
ROW_WORDS = K2 // 2
OUT_ROWS = 768
CHUNK = P
CHUNKS = OUT_ROWS // CHUNK
COLS1 = 2 * CHUNK

FLOPS = 2 * (2 * OUT_ROWS) * K2 * E + 2 * OUT_ROWS * K2 * E


def tile_simplemodel_pc_kernel(tc, h1, cross_w, cross_b, out):
    nc = tc.nc

    x_dram = h1.rearrange("b i (h s) e -> (b i h) (s e)", s=4)
    w_dram = cross_w.rearrange("(u p e) k -> u e p k", u=2, e=2)
    out_dram = out.rearrange("b i h e -> (b i h) e")

    with ExitStack() as ctx:
        const = ctx.enter_context(tc.tile_pool(name="const", bufs=1))
        xin = ctx.enter_context(tc.tile_pool(name="xin", bufs=CHUNKS))
        work = ctx.enter_context(tc.tile_pool(name="work", bufs=3))
        psum = ctx.enter_context(tc.psum_pool(name="psum", bufs=8))

        ident = const.tile([P, P], F32)
        masks.make_identity(nc, ident[:])
        ones = const.tile([P, P], BF16)
        nc.vector.memset(ones[:], 1.0)
        bias_row0 = const.tile([P, E], BF16)
        nc.vector.memset(bias_row0[:].bitcast(I32), 0)

        w_sb = const.tile([P, PACK * K2], BF16)
        x_sb = []
        for c in range(CHUNKS):
            x_rows = xin.tile([P, 2 * K2], BF16)
            x_sb.append(x_rows)

        def load_x(c):
            for j in range(2):
                k_range = slice(j * K2, (j + 1) * K2)
                nc.sync.dma_start(
                    out=x_sb[c][:, k_range], in_=x_dram[c * CHUNK : (c + 1) * CHUNK, k_range]
                )

        def load_w(t):
            nc.sync.dma_start(out=w_sb[:, t * K2 : (t + 1) * K2], in_=w_dram[t // 2, t % 2])

        load_x(0)
        load_w(0)
        load_w(1)
        nc.sync.dma_start(out=bias_row0[0:1, :], in_=cross_b.unsqueeze(0))
        load_w(2)
        load_w(3)
        for c in range(1, CHUNKS):
            load_x(c)

        w_grouped = const.tile([P, PASSES * E * PACK], BF16, align_bytes=64)
        w_codes = const.tile([P, PASSES, E], U32, align_bytes=64)
        w_scales = const.tile([P, PASSES, E], U8, align_bytes=64)
        bias_rows = const.tile([P, E], F32)
        bias_cols = const.tile([P, PACK], F32)

        def transpose_rows(words):
            bank = psum.tile([P, PASSES * 2, P], F32, tag="bank")
            for block in range(PASSES * 2):
                nc.tensor.transpose(bank[:, block, :], words[:, block * P : (block + 1) * P], ident[:])
            return bank

        def copy_grouped(copy, grouped, columns, first, bank):
            words = grouped[:].bitcast(F32).rearrange("p (g c u) -> p g c u", g=PASSES, c=columns)
            copy(
                out=words[:, :, first : first + P, :],
                in_=bank[:].rearrange("p (g u) r -> p g r u", g=PASSES),
            )

        t_banks, x_grouped, x_codes, x_scales = {}, {}, {}, {}
        h_banks, h2t, g2_grouped, g2_codes, g2_scales, o_banks = {}, {}, {}, {}, {}, {}

        def transpose_x(c):
            words = x_sb[c][:].bitcast(F32)
            t_banks[c] = [
                transpose_rows(words[:, j * ROW_WORDS : (j + 1) * ROW_WORDS]) for j in range(2)
            ]

        def group_x(c):
            grouped = work.tile([P, PASSES * COLS1 * PACK], BF16, align_bytes=64, name="x_grouped")
            for j in range(2):
                copy_grouped(nc.scalar.copy, grouped, COLS1, j * P, t_banks[c][j])
            x_grouped[c] = grouped

        def quantise_x(c):
            codes = work.tile([P, PASSES, COLS1], U32, align_bytes=64, name="x_codes")
            scales = work.tile([P, PASSES, COLS1], U8, align_bytes=64, name="x_scales")
            nc.vector.quantize_mx(
                out=codes[:].rearrange("p g c -> p (g c)").bitcast(FP8X4),
                scales=scales[:].rearrange("p g c -> p (g c)"),
                in_=x_grouped[c][:],
            )
            x_codes[c], x_scales[c] = codes, scales

        def weight_tile_in(t):
            words = w_sb[:].bitcast(F32)
            bank = transpose_rows(words[:, t * ROW_WORDS : (t + 1) * ROW_WORDS])
            copy = nc.vector.tensor_copy if t % 2 == 0 else nc.scalar.copy
            copy_grouped(copy, w_grouped, E, t * P, bank)

        def quantise_w(t):
            columns = slice(t * P, (t + 1) * P)
            grouped = w_grouped[:].rearrange("p (g c t) -> p g c t", g=PASSES, t=PACK)
            for g in range(PASSES):
                nc.vector.quantize_mx(
                    out=w_codes[:, g, columns].bitcast(FP8X4),
                    scales=w_scales[:, g, columns],
                    in_=grouped[:, g, columns, :].rearrange("p c t -> p (c t)"),
                )

        def level_one(c):
            h_banks[c] = []
            for t in range(PACK):
                columns = slice(t * P, (t + 1) * P)
                bank = psum.tile([P, COLS1], F32, tag="bank", name="h_bank")
                for g in range(PASSES):
                    nc.tensor.matmul_mx(
                        out=bank[:],
                        lhsT=w_codes[:, g, columns].bitcast(FP8X4),
                        lhsT_scale=w_scales[:, g, columns],
                        rhs=x_codes[c][:, g, :].bitcast(FP8X4),
                        rhs_scale=x_scales[c][:, g, :],
                        start=(g == 0),
                        stop=(g == PASSES - 1),
                    )
                h_banks[c].append(bank)

        def add_bias_one(c):
            rounded = work.tile([P, PACK, COLS1], BF16, name="h2t")
            for t in range(PACK):
                nc.scalar.activation(
                    out=rounded[:, t, :],
                    in_=h_banks[c][t][:],
                    func=mybir.ActivationFunctionType.Identity,
                    bias=bias_cols[:, t : t + 1],
                    scale=1.0,
                )
            h2t[c] = rounded

        def group_g2(c):
            grouped = work.tile([P, PASSES, CHUNK * PACK], BF16, align_bytes=64, name="g2_grouped")
            for g in range(PASSES):
                nc.vector.tensor_copy(
                    out=grouped[:, g, :].rearrange("p (c i t) -> p c t i", i=4, t=PACK),
                    in_=h2t[c][:, :, g * CHUNK : (g + 1) * CHUNK].rearrange("p t (c i) -> p c t i", i=4),
                )
            g2_grouped[c] = grouped

        def quantise_g2(c):
            codes = work.tile([P, PASSES, CHUNK], U32, align_bytes=64, name="g2_codes")
            scales = work.tile([P, PASSES, CHUNK], U8, align_bytes=64, name="g2_scales")
            for g in range(PASSES):
                nc.vector.quantize_mx(
                    out=codes[:, g, :].bitcast(FP8X4),
                    scales=scales[:, g, :],
                    in_=g2_grouped[c][:, g, :],
                )
            g2_codes[c], g2_scales[c] = codes, scales

        def level_two(c):
            o_banks[c] = []
            for u in range(2):
                columns = slice(u * HALF_E, (u + 1) * HALF_E)
                bank = psum.tile([P, HALF_E], F32, tag="bank", name="o_bank")
                for g in range(PASSES):
                    nc.tensor.matmul_mx(
                        out=bank[:],
                        lhsT=g2_codes[c][:, g, :].bitcast(FP8X4),
                        lhsT_scale=g2_scales[c][:, g, :],
                        rhs=w_codes[:, g, columns].bitcast(FP8X4),
                        rhs_scale=w_scales[:, g, columns],
                        start=(g == 0),
                        stop=(g == PASSES - 1),
                    )
                o_banks[c].append(bank)

        def finish(c):
            result = work.tile([P, E], F32, name="result")
            for u in range(2):
                columns = slice(u * HALF_E, (u + 1) * HALF_E)
                nc.vector.tensor_tensor(
                    out=result[:, columns].rearrange("p (i e) -> p i e", e=2),
                    in0=o_banks[c][u][:].rearrange("p (e i) -> p i e", e=2),
                    in1=bias_rows[:, columns].rearrange("p (i e) -> p i e", e=2),
                    op=mybir.AluOpType.add,
                )
                nc.sync.dma_start(
                    out=out_dram[c * CHUNK : (c + 1) * CHUNK, columns], in_=result[:, columns]
                )

        def spread_bias():
            spread = psum.tile([P, E], F32, tag="bank")
            nc.tensor.matmul(out=spread[:], lhsT=ones[:], rhs=bias_row0[:], start=True, stop=True)
            nc.scalar.copy(out=bias_rows[:], in_=spread[:])
            turned = psum.tile([P, 2 * P], F32, tag="bank")
            for u in range(2):
                nc.tensor.transpose(
                    turned[:, u * P : (u + 1) * P],
                    bias_row0[:].bitcast(F32)[:, u * P : (u + 1) * P],
                    ident[:],
                )
            nc.vector.tensor_copy(
                out=bias_cols[:].rearrange("p (u e) -> p u e", u=2),
                in_=turned[:].bitcast(BF16).rearrange("p (u c) -> p u c", u=2)[:, :, 0:2],
            )

        transpose_x(0)
        group_x(0)
        weight_tile_in(0)
        quantise_x(0)
        weight_tile_in(1)
        quantise_w(0)
        spread_bias()
        weight_tile_in(2)
        quantise_w(1)
        weight_tile_in(3)
        quantise_w(2)
        transpose_x(1)
        group_x(1)
        quantise_w(3)

        for i in range(CHUNKS + 2):
            if 0 <= i - 1 < CHUNKS:
                quantise_g2(i - 1)
            if 0 <= i - 2 < CHUNKS:
                finish(i - 2)
            if i < CHUNKS:
                level_one(i)
                add_bias_one(i)
            if i + 2 < CHUNKS:
                transpose_x(i + 2)
                group_x(i + 2)
            if 0 <= i - 1 < CHUNKS:
                level_two(i - 1)
            if i + 1 < CHUNKS:
                quantise_x(i + 1)
            if i < CHUNKS:
                group_g2(i)
